import numpy as np
import ml_dtypes


def mxq(x, axis, fmt="e4m3"):
    dtype, down = {"e4m3": (ml_dtypes.float8_e4m3fn, 7), "e5m2": (ml_dtypes.float8_e5m2, 14)}[fmt]
    v = np.moveaxis(np.asarray(x, np.float32).astype(ml_dtypes.bfloat16).astype(np.float64), axis, -1)
    blocks = v.reshape(v.shape[:-1] + (-1, 32))
    amax = np.abs(blocks).max(-1, keepdims=True)
    byte = np.maximum(np.where(amax > 0, np.frexp(amax)[1] - 1 + 127, 0) - down, 1)
    scale = np.exp2(byte - 127.0)
    codes = (blocks / scale).astype(np.float32).astype(dtype).astype(np.float64)
    return np.moveaxis((codes * scale).reshape(v.shape), -1, axis)


WIDE = False


def mx_kscale(k):
    if not WIDE:
        return np.ones(k)
    levels = np.array([10, -10, 5, -5, 0])
    a = np.random.permutation(np.resize(levels, k // 512 * 4)).reshape(k // 512, 4)
    idx = np.arange(k)
    return np.exp2(a[idx // 512, idx % 128 // 32])


BF16 = ml_dtypes.bfloat16


def bf(x):
    return np.asarray(x, np.float32).astype(BF16)


def f64(x):
    return np.asarray(x).astype(np.float64)


E2M1 = np.array([0.0, 0.5, 1.0, 1.5, 2.0, 3.0, 4.0, 6.0, -0.0, -0.5, -1.0, -1.5, -2.0, -3.0, -4.0, -6.0])


def pack_weight(w, fmt):
    k, n = w.shape
    w = f64(bf(w)).reshape(k // 32, 32, n)
    amax = np.abs(w).max(1)
    if fmt == "e4m3":
        byte = np.frexp(amax)[1] - 1 + 127 - 7
    else:
        mant, ex = np.frexp(amax / 6.0)
        byte = np.where(mant > 0.5, ex, ex - 1) + 127
    byte = np.clip(np.where(amax > 0, byte, 1), 1, 254)
    scaled = (w * np.exp2(127.0 - byte)[:, None, :]).reshape(k, n).astype(np.float32)
    by_word = np.ascontiguousarray(scaled.reshape(k // 512, 128, 4, n).transpose(0, 1, 3, 2))
    if fmt == "e4m3":
        words = by_word.astype(ml_dtypes.float8_e4m3fn).view(np.uint8)
    else:
        c = by_word.astype(ml_dtypes.float4_e2m1fn).view(np.uint8) & 0xF
        words = c[..., 0::2] | (c[..., 1::2] << 4)
    return np.ascontiguousarray(words), np.ascontiguousarray(byte.astype(np.uint8).reshape(k // 512, 16, n))


def unpack_weight(words, scales, fmt):
    g, p, n, _ = words.shape
    if fmt == "e4m3":
        vals = np.ascontiguousarray(words).view(ml_dtypes.float8_e4m3fn).astype(np.float64)
    else:
        nib = np.empty((g, p, n, 4), np.uint8)
        nib[..., 0::2] = words & 0xF
        nib[..., 1::2] = words >> 4
        vals = E2M1[nib]
    vals = vals * np.repeat(np.exp2(scales.astype(np.float64) - 127.0), 8, axis=1)[..., None]
    return vals.transpose(0, 1, 3, 2).reshape(g * 512, n)

def pack4(w):
    words, scales = pack_weight(w, "e2m1")
    return words.reshape(words.shape[0], 128, -1), scales


def unpack4(words, scales):
    return unpack_weight(words.reshape(words.shape[0], 128, -1, 2), scales, "e2m1")


B, N, C, H = 4, 1024, 512, 16
EPS = 1e-6


def rmsnorm(v, w):
    var = np.mean(np.square(v), axis=-1, keepdims=True)
    return v * (1.0 / np.sqrt(var + EPS)) * w


def setup_inputs():
    s = mx_kscale(C)
    x = bf(np.random.standard_normal((B, N, C)) * s)
    w = np.random.standard_normal((3 * C, C)) / np.sqrt(C) / s[None, :]
    words, scales = pack4(np.ascontiguousarray(w.T))
    q_norm_w = bf(1.0 + 0.1 * np.random.standard_normal(C))
    k_norm_w = bf(1.0 + 0.1 * np.random.standard_normal(C))
    return {"x": x,
            "w_qkv_words": words,
            "w_qkv_scales": scales,
            "q_norm_w": q_norm_w,
            "k_norm_w": k_norm_w}


def reference(x, w_qkv_words, w_qkv_scales, q_norm_w, k_norm_w):
    xq = mxq(f64(x), 2, "e4m3")
    wt = unpack4(w_qkv_words, w_qkv_scales)
    q = xq @ wt[:, :C]
    k = xq @ wt[:, C:2 * C]
    v = xq @ wt[:, 2 * C:]
    return rmsnorm(q, f64(q_norm_w)), rmsnorm(k, f64(k_norm_w)), v

@@ -1,0 +1,186 @@
+from contextlib import ExitStack
+
+import concourse.mybir as mybir
+from concourse.masks import make_identity
+
+F32 = mybir.dt.float32
+BF16 = mybir.dt.bfloat16
+I32 = mybir.dt.int32
+U32 = mybir.dt.uint32
+U8 = mybir.dt.uint8
+FP8X4 = mybir.dt.float8_e4m3fn_x4
+FP4X4 = mybir.dt.float4_e2m1fn_x4
+ACT = mybir.ActivationFunctionType
+ALU = mybir.AluOpType
+
+P = 128
+C = 512
+TOKENS = 4 * 1024
+EPS = 1e-6
+ROWS = 4
+GROUP = P * ROWS
+GROUPS = TOKENS // GROUP
+PAIR = 2
+PAIRS = TOKENS // (PAIR * P)
+AHEAD = 2
+Q, K, V = 0, 1, 2
+
+FLOPS = 2 * TOKENS * C * 3 * C
+
+
+def tile_internattention_pa_t_kernel(
+    tc, x, w_qkv_words, w_qkv_scales, q_norm_w, k_norm_w, out_0, out_1, out_2
+):
+    nc = tc.nc
+    x_groups = x.flatten_outer_dims().rearrange("(g p j) c -> g p j c", p=P, j=ROWS)
+    out_groups = [
+        o.flatten_outer_dims().rearrange("(g p j) c -> g p j c", p=P, j=ROWS)
+        for o in (out_0, out_1, out_2)
+    ]
+
+    with ExitStack() as stack:
+        stack.enter_context(tc.manual_schedule())
+        const = stack.enter_context(tc.tile_pool(name="const", bufs=1))
+        x_pool = stack.enter_context(tc.tile_pool(name="x", bufs=GROUPS))
+        grouped_pool = stack.enter_context(tc.tile_pool(name="grouped", bufs=2))
+        mx_pool = stack.enter_context(tc.tile_pool(name="mx", bufs=AHEAD + 2))
+        stat_pool = stack.enter_context(tc.tile_pool(name="stat", bufs=4))
+        out_pool = stack.enter_context(tc.tile_pool(name="out", bufs=4))
+        psum = stack.enter_context(tc.psum_pool(name="psum", bufs=2))
+
+        w_words = const.tile([P, 2 * 3 * C], U8, align_bytes=64)
+        w_plane = const.tile([P, 3 * C], U8, align_bytes=64)
+        gain_rows = const.tile([P, 2 * C], BF16)
+        ones = const.tile([P, P], BF16)
+        gains = const.tile([P, 2, C], F32)
+        ident = const.tile([P, P], F32)
+        one_col = const.tile([P, 1], F32)
+
+        nc.vector.memset(w_plane[:].bitcast(I32), 0)
+        nc.vector.memset(gain_rows[:], 0.0)
+        nc.vector.memset(ones[:], 1.0)
+        nc.vector.memset(one_col[:], 1.0)
+        make_identity(nc, ident[:])
+        nc.scalar.activation(out=one_col[:], in_=one_col[:], func=ACT.Sqrt)
+
+        x_sb = []
+        for g in range(GROUPS):
+            x_g = x_pool.tile([P, ROWS, C], BF16, name="x_g")
+            nc.sync.dma_start(out=x_g[:], in_=x_groups[g])
+            x_sb.append(x_g)
+            if g == 0:
+                for quad in range(4):
+                    nc.sync.dma_start(
+                        out=w_plane[32 * quad : 32 * quad + 4, :].bitcast(I32),
+                        in_=w_qkv_scales[0, 4 * quad : 4 * quad + 4, :].bitcast(I32),
+                    )
+                nc.sync.dma_start(out=w_words[:].bitcast(I32), in_=w_qkv_words[0].bitcast(I32))
+        nc.scalar.dma_start(out=gain_rows[0:1, 0:C], in_=q_norm_w.unsqueeze(0))
+        nc.scalar.dma_start(out=gain_rows[0:1, C : 2 * C], in_=k_norm_w.unsqueeze(0))
+
+        for o in (Q, K):
+            gain_ps = psum.tile([P, C], F32, name="gain_ps", tag="acc%d" % o)
+            nc.tensor.matmul(
+                out=gain_ps[:], lhsT=ones[:], rhs=gain_rows[:, C * o : C * (o + 1)],
+                start=True, stop=True,
+            )
+            nc.scalar.copy(out=gains[:, o, :], in_=gain_ps[:])
+
+        def transpose_pair(h):
+            g, half = divmod(h, ROWS // PAIR)
+            xt = psum.tile([P, PAIR, 2, P], F32, name="xt")
+            for i in range(PAIR):
+                words = x_sb[g][:, PAIR * half + i, :].bitcast(F32)
+                for u in range(2):
+                    nc.tensor.transpose(xt[:, i, u, :], words[:, u : C // 2 : 2], ident[:])
+            return xt
+
+        def regroup_pair(xt):
+            grouped = grouped_pool.tile([P, PAIR, P, 4], BF16, name="grouped", align_bytes=64)
+            nc.vector.tensor_copy(
+                out=grouped[:].bitcast(F32), in_=xt[:].rearrange("p i u r -> p i r u")
+            )
+            return grouped
+
+        def quantise_pair(grouped):
+            codes = mx_pool.tile([P, PAIR * P], U32, name="codes", align_bytes=64)
+            plane = mx_pool.tile([P, PAIR * P], U8, name="plane", align_bytes=64)
+            nc.vector.quantize_mx(
+                out=codes[:].bitcast(FP8X4),
+                scales=plane[:],
+                in_=grouped[:].rearrange("p i r t -> p (i r t)"),
+            )
+            return codes, plane
+
+        def token_tile(codes, plane, i, out_sb, j):
+            tokens = slice(P * i, P * (i + 1))
+            acc = []
+            for o in (Q, K, V):
+                acc_o = psum.tile([P, C], F32, name="acc_o", tag="acc%d" % o)
+                nc.tensor.matmul_mx(
+                    out=acc_o[:],
+                    lhsT=codes[:, tokens].bitcast(FP8X4),
+                    lhsT_scale=plane[:, tokens],
+                    rhs=w_words[:, 2 * C * o : 2 * C * (o + 1)].bitcast(FP4X4),
+                    rhs_scale=w_plane[:, C * o : C * (o + 1)],
+                    start=True,
+                    stop=True,
+                )
+                acc.append(acc_o)
+            sumsq = stat_pool.tile([P, 2], F32, name="sumsq")
+            for o in (Q, K):
+                squares = stat_pool.tile([P, C], BF16, name="squares")
+                nc.scalar.activation(
+                    out=squares[:], in_=acc[o][:], func=ACT.Square, accum_out=sumsq[:, o : o + 1]
+                )
+            rms = stat_pool.tile([P, 2], F32, name="rms")
+            nc.scalar.activation(out=rms[:], in_=sumsq[:], func=ACT.Sqrt, scale=1.0 / C, bias=EPS)
+            if j == 0:
+                nc.vector.tensor_copy(out=out_sb[V][:, j, :], in_=acc[V][:])
+            else:
+                nc.scalar.copy(out=out_sb[V][:, j, :], in_=acc[V][:])
+            rstd = stat_pool.tile([P, 2], F32, name="rstd")
+            nc.vector.reciprocal(out=rstd[:], in_=rms[:])
+            for o in (Q, K):
+                nc.vector.scalar_tensor_tensor(
+                    out=out_sb[o][:, j, :],
+                    in0=acc[o][:],
+                    scalar=rstd[:, o : o + 1],
+                    in1=gains[:, o, :],
+                    op0=ALU.mult,
+                    op1=ALU.mult,
+                )
+
+        def store_rows(g, out_sb, rows):
+            for o in (V, Q, K):
+                nc.sync.dma_start(out=out_groups[o][g][:, rows, :], in_=out_sb[o][:, rows, :])
+
+        def store_after_tile(g, out_sb, j):
+            if g == 0 or g == GROUPS - 1:
+                store_rows(g, out_sb, slice(j, j + 1))
+            elif j == ROWS - 1:
+                store_rows(g, out_sb, slice(0, ROWS))
+
+        quantised = {}
+        for h in range(AHEAD):
+            quantised[h] = quantise_pair(regroup_pair(transpose_pair(h)))
+
+        out_sb = None
+        for h in range(PAIRS):
+            g, half = divmod(h, ROWS // PAIR)
+            if half == 0:
+                out_sb = [
+                    out_pool.tile([P, ROWS, C], F32, name="out_sb%d" % o) for o in (Q, K, V)
+                ]
+            codes, plane = quantised[h]
+            later = h + AHEAD
+            if later < PAIRS:
+                xt = transpose_pair(later)
+            token_tile(codes, plane, 0, out_sb, PAIR * half)
+            store_after_tile(g, out_sb, PAIR * half)
+            if later < PAIRS:
+                grouped = regroup_pair(xt)
+            token_tile(codes, plane, 1, out_sb, PAIR * half + 1)
+            store_after_tile(g, out_sb, PAIR * half + 1)
+            if later < PAIRS:
+                quantised[later] = quantise_pair(grouped)

@@ -17,13 +17,11 @@ P = 128
 C = 512
 TOKENS = 4 * 1024
 EPS = 1e-6
-ROWS = 4
-GROUP = P * ROWS
-GROUPS = TOKENS // GROUP
 PAIR = 2
 PAIRS = TOKENS // (PAIR * P)
 AHEAD = 2
 Q, K, V = 0, 1, 2
+ACC_BANKS = 7
 
 FLOPS = 2 * TOKENS * C * 3 * C
 
@@ -32,21 +30,21 @@ def tile_internattention_pa_t_kernel(
     tc, x, w_qkv_words, w_qkv_scales, q_norm_w, k_norm_w, out_0, out_1, out_2
 ):
     nc = tc.nc
-    x_groups = x.flatten_outer_dims().rearrange("(g p j) c -> g p j c", p=P, j=ROWS)
-    out_groups = [
-        o.flatten_outer_dims().rearrange("(g p j) c -> g p j c", p=P, j=ROWS)
+    x_pairs = x.flatten_outer_dims().rearrange("(h p i) c -> h p i c", p=P, i=PAIR)
+    out_pairs = [
+        o.flatten_outer_dims().rearrange("(h p i) c -> h p i c", p=P, i=PAIR)
         for o in (out_0, out_1, out_2)
     ]
 
     with ExitStack() as stack:
         stack.enter_context(tc.manual_schedule())
         const = stack.enter_context(tc.tile_pool(name="const", bufs=1))
-        x_pool = stack.enter_context(tc.tile_pool(name="x", bufs=GROUPS))
+        x_pool = stack.enter_context(tc.tile_pool(name="x", bufs=PAIRS))
         grouped_pool = stack.enter_context(tc.tile_pool(name="grouped", bufs=2))
         mx_pool = stack.enter_context(tc.tile_pool(name="mx", bufs=AHEAD + 2))
         stat_pool = stack.enter_context(tc.tile_pool(name="stat", bufs=4))
-        out_pool = stack.enter_context(tc.tile_pool(name="out", bufs=4))
-        psum = stack.enter_context(tc.psum_pool(name="psum", bufs=2))
+        out_pool = stack.enter_context(tc.tile_pool(name="out", bufs=6))
+        psum = stack.enter_context(tc.psum_pool(name="psum", bufs=1))
 
         w_words = const.tile([P, 2 * 3 * C], U8, align_bytes=64)
         w_plane = const.tile([P, 3 * C], U8, align_bytes=64)
@@ -56,30 +54,30 @@ def tile_internattention_pa_t_kernel(
         ident = const.tile([P, P], F32)
         one_col = const.tile([P, 1], F32)
 
-        nc.vector.memset(w_plane[:].bitcast(I32), 0)
         nc.vector.memset(gain_rows[:], 0.0)
+        nc.vector.memset(w_plane[:].bitcast(I32), 0)
         nc.vector.memset(ones[:], 1.0)
         nc.vector.memset(one_col[:], 1.0)
         make_identity(nc, ident[:])
-        nc.scalar.activation(out=one_col[:], in_=one_col[:], func=ACT.Sqrt)
+        nc.scalar.activation(out=one_col[:], in_=one_col[:], func=ACT.Abs_reciprocal_sqrt)
 
+        nc.sync.dma_start(out=gain_rows[0:1, 0:C], in_=q_norm_w.unsqueeze(0))
+        nc.sync.dma_start(out=gain_rows[0:1, C : 2 * C], in_=k_norm_w.unsqueeze(0))
         x_sb = []
-        for g in range(GROUPS):
-            x_g = x_pool.tile([P, ROWS, C], BF16, name="x_g")
-            nc.sync.dma_start(out=x_g[:], in_=x_groups[g])
-            x_sb.append(x_g)
-            if g == 0:
+        for h in range(PAIRS):
+            x_h = x_pool.tile([P, PAIR, C], BF16, name="x_h")
+            nc.sync.dma_start(out=x_h[:], in_=x_pairs[h])
+            x_sb.append(x_h)
+            if h == 0:
                 for quad in range(4):
                     nc.sync.dma_start(
                         out=w_plane[32 * quad : 32 * quad + 4, :].bitcast(I32),
                         in_=w_qkv_scales[0, 4 * quad : 4 * quad + 4, :].bitcast(I32),
                     )
                 nc.sync.dma_start(out=w_words[:].bitcast(I32), in_=w_qkv_words[0].bitcast(I32))
-        nc.scalar.dma_start(out=gain_rows[0:1, 0:C], in_=q_norm_w.unsqueeze(0))
-        nc.scalar.dma_start(out=gain_rows[0:1, C : 2 * C], in_=k_norm_w.unsqueeze(0))
 
         for o in (Q, K):
-            gain_ps = psum.tile([P, C], F32, name="gain_ps", tag="acc%d" % o)
+            gain_ps = psum.tile([P, C], F32, name="gain_ps", tag="acc", bufs=ACC_BANKS)
             nc.tensor.matmul(
                 out=gain_ps[:], lhsT=ones[:], rhs=gain_rows[:, C * o : C * (o + 1)],
                 start=True, stop=True,
@@ -87,10 +85,9 @@ def tile_internattention_pa_t_kernel(
             nc.scalar.copy(out=gains[:, o, :], in_=gain_ps[:])
 
         def transpose_pair(h):
-            g, half = divmod(h, ROWS // PAIR)
             xt = psum.tile([P, PAIR, 2, P], F32, name="xt")
             for i in range(PAIR):
-                words = x_sb[g][:, PAIR * half + i, :].bitcast(F32)
+                words = x_sb[h][:, i, :].bitcast(F32)
                 for u in range(2):
                     nc.tensor.transpose(xt[:, i, u, :], words[:, u : C // 2 : 2], ident[:])
             return xt
@@ -112,11 +109,11 @@ def tile_internattention_pa_t_kernel(
             )
             return codes, plane
 
-        def token_tile(codes, plane, i, out_sb, j):
+        def token_tile(codes, plane, i, out_sb, v_on_vector):
             tokens = slice(P * i, P * (i + 1))
             acc = []
             for o in (Q, K, V):
-                acc_o = psum.tile([P, C], F32, name="acc_o", tag="acc%d" % o)
+                acc_o = psum.tile([P, C], F32, name="acc_o", tag="acc", bufs=ACC_BANKS)
                 nc.tensor.matmul_mx(
                     out=acc_o[:],
                     lhsT=codes[:, tokens].bitcast(FP8X4),
@@ -133,17 +130,17 @@ def tile_internattention_pa_t_kernel(
                 nc.scalar.activation(
                     out=squares[:], in_=acc[o][:], func=ACT.Square, accum_out=sumsq[:, o : o + 1]
                 )
-            rms = stat_pool.tile([P, 2], F32, name="rms")
-            nc.scalar.activation(out=rms[:], in_=sumsq[:], func=ACT.Sqrt, scale=1.0 / C, bias=EPS)
-            if j == 0:
-                nc.vector.tensor_copy(out=out_sb[V][:, j, :], in_=acc[V][:])
+            if v_on_vector:
+                nc.vector.tensor_copy(out=out_sb[V][:, i, :], in_=acc[V][:])
             else:
-                nc.scalar.copy(out=out_sb[V][:, j, :], in_=acc[V][:])
+                nc.scalar.copy(out=out_sb[V][:, i, :], in_=acc[V][:])
             rstd = stat_pool.tile([P, 2], F32, name="rstd")
-            nc.vector.reciprocal(out=rstd[:], in_=rms[:])
+            nc.scalar.activation(
+                out=rstd[:], in_=sumsq[:], func=ACT.Abs_reciprocal_sqrt, scale=1.0 / C, bias=EPS
+            )
             for o in (Q, K):
                 nc.vector.scalar_tensor_tensor(
-                    out=out_sb[o][:, j, :],
+                    out=out_sb[o][:, i, :],
                     in0=acc[o][:],
                     scalar=rstd[:, o : o + 1],
                     in1=gains[:, o, :],
@@ -151,36 +148,19 @@ def tile_internattention_pa_t_kernel(
                     op1=ALU.mult,
                 )
 
-        def store_rows(g, out_sb, rows):
-            for o in (V, Q, K):
-                nc.sync.dma_start(out=out_groups[o][g][:, rows, :], in_=out_sb[o][:, rows, :])
-
-        def store_after_tile(g, out_sb, j):
-            if g == 0 or g == GROUPS - 1:
-                store_rows(g, out_sb, slice(j, j + 1))
-            elif j == ROWS - 1:
-                store_rows(g, out_sb, slice(0, ROWS))
-
         quantised = {}
         for h in range(AHEAD):
             quantised[h] = quantise_pair(regroup_pair(transpose_pair(h)))
 
-        out_sb = None
         for h in range(PAIRS):
-            g, half = divmod(h, ROWS // PAIR)
-            if half == 0:
-                out_sb = [
-                    out_pool.tile([P, ROWS, C], F32, name="out_sb%d" % o) for o in (Q, K, V)
-                ]
+            out_sb = [out_pool.tile([P, PAIR, C], F32, name="out_sb%d" % o) for o in (Q, K, V)]
             codes, plane = quantised[h]
             later = h + AHEAD
+            token_tile(codes, plane, 0, out_sb, False)
             if later < PAIRS:
-                xt = transpose_pair(later)
-            token_tile(codes, plane, 0, out_sb, PAIR * half)
-            store_after_tile(g, out_sb, PAIR * half)
-            if later < PAIRS:
-                grouped = regroup_pair(xt)
-            token_tile(codes, plane, 1, out_sb, PAIR * half + 1)
-            store_after_tile(g, out_sb, PAIR * half + 1)
+                grouped = regroup_pair(transpose_pair(later))
+            token_tile(codes, plane, 1, out_sb, h % 2 == 0)
             if later < PAIRS:
                 quantised[later] = quantise_pair(grouped)
+            for o in (V, Q, K):
+                nc.sync.dma_start(out=out_pairs[o][h], in_=out_sb[o][:])

@@ -61,14 +61,14 @@ def tile_internattention_pa_t_kernel(
         make_identity(nc, ident[:])
         nc.scalar.activation(out=one_col[:], in_=one_col[:], func=ACT.Abs_reciprocal_sqrt)
 
-        nc.sync.dma_start(out=gain_rows[0:1, 0:C], in_=q_norm_w.unsqueeze(0))
-        nc.sync.dma_start(out=gain_rows[0:1, C : 2 * C], in_=k_norm_w.unsqueeze(0))
         x_sb = []
         for h in range(PAIRS):
             x_h = x_pool.tile([P, PAIR, C], BF16, name="x_h")
             nc.sync.dma_start(out=x_h[:], in_=x_pairs[h])
             x_sb.append(x_h)
             if h == 0:
+                nc.sync.dma_start(out=gain_rows[0:1, 0:C], in_=q_norm_w.unsqueeze(0))
+                nc.sync.dma_start(out=gain_rows[0:1, C : 2 * C], in_=k_norm_w.unsqueeze(0))
                 for quad in range(4):
                     nc.sync.dma_start(
                         out=w_plane[32 * quad : 32 * quad + 4, :].bitcast(I32),
@@ -76,13 +76,14 @@ def tile_internattention_pa_t_kernel(
                     )
                 nc.sync.dma_start(out=w_words[:].bitcast(I32), in_=w_qkv_words[0].bitcast(I32))
 
-        for o in (Q, K):
-            gain_ps = psum.tile([P, C], F32, name="gain_ps", tag="acc", bufs=ACC_BANKS)
-            nc.tensor.matmul(
-                out=gain_ps[:], lhsT=ones[:], rhs=gain_rows[:, C * o : C * (o + 1)],
-                start=True, stop=True,
-            )
-            nc.scalar.copy(out=gains[:, o, :], in_=gain_ps[:])
+        def spread_gains():
+            for o in (Q, K):
+                gain_ps = psum.tile([P, C], F32, name="gain_ps", tag="acc", bufs=ACC_BANKS)
+                nc.tensor.matmul(
+                    out=gain_ps[:], lhsT=ones[:], rhs=gain_rows[:, C * o : C * (o + 1)],
+                    start=True, stop=True,
+                )
+                nc.scalar.copy(out=gains[:, o, :], in_=gain_ps[:])
 
         def transpose_pair(h):
             xt = psum.tile([P, PAIR, 2, P], F32, name="xt")
@@ -109,10 +110,10 @@ def tile_internattention_pa_t_kernel(
             )
             return codes, plane
 
-        def token_tile(codes, plane, i, out_sb, v_on_vector):
+        def multiply(codes, plane, i, outputs):
             tokens = slice(P * i, P * (i + 1))
             acc = []
-            for o in (Q, K, V):
+            for o in outputs:
                 acc_o = psum.tile([P, C], F32, name="acc_o", tag="acc", bufs=ACC_BANKS)
                 nc.tensor.matmul_mx(
                     out=acc_o[:],
@@ -124,6 +125,9 @@ def tile_internattention_pa_t_kernel(
                     stop=True,
                 )
                 acc.append(acc_o)
+            return acc
+
+        def norm_and_copy(acc, i, out_sb, v_on_vector):
             sumsq = stat_pool.tile([P, 2], F32, name="sumsq")
             for o in (Q, K):
                 squares = stat_pool.tile([P, C], BF16, name="squares")
@@ -148,19 +152,30 @@ def tile_internattention_pa_t_kernel(
                     op1=ALU.mult,
                 )
 
+        def store(h, out_sb, rows):
+            for o in (V, Q, K):
+                nc.sync.dma_start(out=out_pairs[o][h][:, rows, :], in_=out_sb[o][:, rows, :])
+
         quantised = {}
         for h in range(AHEAD):
-            quantised[h] = quantise_pair(regroup_pair(transpose_pair(h)))
+            grouped = regroup_pair(transpose_pair(h))
+            if h == 0:
+                spread_gains()
+            quantised[h] = quantise_pair(grouped)
 
         for h in range(PAIRS):
             out_sb = [out_pool.tile([P, PAIR, C], F32, name="out_sb%d" % o) for o in (Q, K, V)]
             codes, plane = quantised[h]
             later = h + AHEAD
-            token_tile(codes, plane, 0, out_sb, False)
+            norm_and_copy(multiply(codes, plane, 0, (Q, K, V)), 0, out_sb, False)
+            last = h == PAIRS - 1
+            if last:
+                store(h, out_sb, slice(0, 1))
+            acc = multiply(codes, plane, 1, (Q,))
             if later < PAIRS:
                 grouped = regroup_pair(transpose_pair(later))
-            token_tile(codes, plane, 1, out_sb, h % 2 == 0)
+            acc.extend(multiply(codes, plane, 1, (K, V)))
+            norm_and_copy(acc, 1, out_sb, h % 2 == 0)
             if later < PAIRS:
                 quantised[later] = quantise_pair(grouped)
-            for o in (V, Q, K):
-                nc.sync.dma_start(out=out_pairs[o][h], in_=out_sb[o][:])
+            store(h, out_sb, slice(1, PAIR) if last else slice(0, PAIR))

@@ -19,6 +19,7 @@ TOKENS = 4 * 1024
 EPS = 1e-6
 PAIR = 2
 PAIRS = TOKENS // (PAIR * P)
+GROUP = 2
 AHEAD = 2
 Q, K, V = 0, 1, 2
 ACC_BANKS = 7
@@ -30,16 +31,16 @@ def tile_internattention_pa_t_kernel(
     tc, x, w_qkv_words, w_qkv_scales, q_norm_w, k_norm_w, out_0, out_1, out_2
 ):
     nc = tc.nc
-    x_pairs = x.flatten_outer_dims().rearrange("(h p i) c -> h p i c", p=P, i=PAIR)
+    x_groups = x.flatten_outer_dims().rearrange("(g p r) c -> g p r c", p=P, r=GROUP * PAIR)
     out_pairs = [
-        o.flatten_outer_dims().rearrange("(h p i) c -> h p i c", p=P, i=PAIR)
+        o.flatten_outer_dims().rearrange("(g p a i) c -> g a p i c", p=P, a=GROUP, i=PAIR)
         for o in (out_0, out_1, out_2)
     ]
 
     with ExitStack() as stack:
         stack.enter_context(tc.manual_schedule())
         const = stack.enter_context(tc.tile_pool(name="const", bufs=1))
-        x_pool = stack.enter_context(tc.tile_pool(name="x", bufs=PAIRS))
+        x_pool = stack.enter_context(tc.tile_pool(name="x", bufs=PAIRS // GROUP))
         grouped_pool = stack.enter_context(tc.tile_pool(name="grouped", bufs=2))
         mx_pool = stack.enter_context(tc.tile_pool(name="mx", bufs=AHEAD + 2))
         stat_pool = stack.enter_context(tc.tile_pool(name="stat", bufs=4))
@@ -62,11 +63,13 @@ def tile_internattention_pa_t_kernel(
         nc.scalar.activation(out=one_col[:], in_=one_col[:], func=ACT.Abs_reciprocal_sqrt)
 
         x_sb = []
-        for h in range(PAIRS):
-            x_h = x_pool.tile([P, PAIR, C], BF16, name="x_h")
-            nc.sync.dma_start(out=x_h[:], in_=x_pairs[h])
-            x_sb.append(x_h)
-            if h == 0:
+        for g in range(PAIRS // GROUP):
+            x_g = x_pool.tile([P, GROUP * PAIR, C], BF16, name="x_g")
+            x_sb.append(x_g)
+            if g > 0:
+                nc.sync.dma_start(out=x_g[:], in_=x_groups[g])
+            else:
+                nc.sync.dma_start(out=x_g[:, 0:PAIR, :], in_=x_groups[g][:, 0:PAIR, :])
                 nc.sync.dma_start(out=gain_rows[0:1, 0:C], in_=q_norm_w.unsqueeze(0))
                 nc.sync.dma_start(out=gain_rows[0:1, C : 2 * C], in_=k_norm_w.unsqueeze(0))
                 for quad in range(4):
@@ -75,6 +78,7 @@ def tile_internattention_pa_t_kernel(
                         in_=w_qkv_scales[0, 4 * quad : 4 * quad + 4, :].bitcast(I32),
                     )
                 nc.sync.dma_start(out=w_words[:].bitcast(I32), in_=w_qkv_words[0].bitcast(I32))
+                nc.sync.dma_start(out=x_g[:, PAIR:, :], in_=x_groups[g][:, PAIR:, :])
 
         def spread_gains():
             for o in (Q, K):
@@ -88,7 +92,7 @@ def tile_internattention_pa_t_kernel(
         def transpose_pair(h):
             xt = psum.tile([P, PAIR, 2, P], F32, name="xt")
             for i in range(PAIR):
-                words = x_sb[h][:, i, :].bitcast(F32)
+                words = x_sb[h // GROUP][:, PAIR * (h % GROUP) + i, :].bitcast(F32)
                 for u in range(2):
                     nc.tensor.transpose(xt[:, i, u, :], words[:, u : C // 2 : 2], ident[:])
             return xt
@@ -154,7 +158,9 @@ def tile_internattention_pa_t_kernel(
 
         def store(h, out_sb, rows):
             for o in (V, Q, K):
-                nc.sync.dma_start(out=out_pairs[o][h][:, rows, :], in_=out_sb[o][:, rows, :])
+                nc.sync.dma_start(
+                    out=out_pairs[o][h // GROUP, h % GROUP][:, rows, :], in_=out_sb[o][:, rows, :]
+                )
 
         quantised = {}
         for h in range(AHEAD):

@@ -19,7 +19,10 @@ TOKENS = 4 * 1024
 EPS = 1e-6
 PAIR = 2
 PAIRS = TOKENS // (PAIR * P)
-GROUP = 2
+TILES = TOKENS // P
+LOAD_PLAN = (2, 2, 4, 8, 8, 8)
+STORE_PLAN = (2, 2, 4, 4, 4, 4, 4, 4, 2, 1, 1)
+STORE_MAX = max(STORE_PLAN)
 AHEAD = 2
 Q, K, V = 0, 1, 2
 ACC_BANKS = 7
@@ -31,20 +34,19 @@ def tile_internattention_pa_t_kernel(
     tc, x, w_qkv_words, w_qkv_scales, q_norm_w, k_norm_w, out_0, out_1, out_2
 ):
     nc = tc.nc
-    x_groups = x.flatten_outer_dims().rearrange("(g p r) c -> g p r c", p=P, r=GROUP * PAIR)
-    out_pairs = [
-        o.flatten_outer_dims().rearrange("(g p a i) c -> g a p i c", p=P, a=GROUP, i=PAIR)
-        for o in (out_0, out_1, out_2)
+    x_rows = x.flatten_outer_dims().rearrange("(p r) c -> p r c", p=P)
+    out_rows = [
+        o.flatten_outer_dims().rearrange("(p r) c -> p r c", p=P) for o in (out_0, out_1, out_2)
     ]
 
     with ExitStack() as stack:
         stack.enter_context(tc.manual_schedule())
         const = stack.enter_context(tc.tile_pool(name="const", bufs=1))
-        x_pool = stack.enter_context(tc.tile_pool(name="x", bufs=PAIRS // GROUP))
+        x_pool = stack.enter_context(tc.tile_pool(name="x", bufs=1))
         grouped_pool = stack.enter_context(tc.tile_pool(name="grouped", bufs=2))
         mx_pool = stack.enter_context(tc.tile_pool(name="mx", bufs=AHEAD + 2))
         stat_pool = stack.enter_context(tc.tile_pool(name="stat", bufs=4))
-        out_pool = stack.enter_context(tc.tile_pool(name="out", bufs=6))
+        out_pool = stack.enter_context(tc.tile_pool(name="out", bufs=5))
         psum = stack.enter_context(tc.psum_pool(name="psum", bufs=1))
 
         w_words = const.tile([P, 2 * 3 * C], U8, align_bytes=64)
@@ -63,13 +65,12 @@ def tile_internattention_pa_t_kernel(
         nc.scalar.activation(out=one_col[:], in_=one_col[:], func=ACT.Abs_reciprocal_sqrt)
 
         x_sb = []
-        for g in range(PAIRS // GROUP):
-            x_g = x_pool.tile([P, GROUP * PAIR, C], BF16, name="x_g")
-            x_sb.append(x_g)
-            if g > 0:
-                nc.sync.dma_start(out=x_g[:], in_=x_groups[g])
-            else:
-                nc.sync.dma_start(out=x_g[:, 0:PAIR, :], in_=x_groups[g][:, 0:PAIR, :])
+        for j, n in enumerate(LOAD_PLAN):
+            first = len(x_sb)
+            x_j = x_pool.tile([P, n, C], BF16, name="x_%d" % j)
+            nc.sync.dma_start(out=x_j[:], in_=x_rows[:, first : first + n, :])
+            x_sb.extend([x_j[:, i, :] for i in range(n)])
+            if j == 0:
                 nc.sync.dma_start(out=gain_rows[0:1, 0:C], in_=q_norm_w.unsqueeze(0))
                 nc.sync.dma_start(out=gain_rows[0:1, C : 2 * C], in_=k_norm_w.unsqueeze(0))
                 for quad in range(4):
@@ -78,7 +79,6 @@ def tile_internattention_pa_t_kernel(
                         in_=w_qkv_scales[0, 4 * quad : 4 * quad + 4, :].bitcast(I32),
                     )
                 nc.sync.dma_start(out=w_words[:].bitcast(I32), in_=w_qkv_words[0].bitcast(I32))
-                nc.sync.dma_start(out=x_g[:, PAIR:, :], in_=x_groups[g][:, PAIR:, :])
 
         def spread_gains():
             for o in (Q, K):
@@ -92,7 +92,7 @@ def tile_internattention_pa_t_kernel(
         def transpose_pair(h):
             xt = psum.tile([P, PAIR, 2, P], F32, name="xt")
             for i in range(PAIR):
-                words = x_sb[h // GROUP][:, PAIR * (h % GROUP) + i, :].bitcast(F32)
+                words = x_sb[PAIR * h + i].bitcast(F32)
                 for u in range(2):
                     nc.tensor.transpose(xt[:, i, u, :], words[:, u : C // 2 : 2], ident[:])
             return xt
@@ -131,7 +131,7 @@ def tile_internattention_pa_t_kernel(
                 acc.append(acc_o)
             return acc
 
-        def norm_and_copy(acc, i, out_sb, v_on_vector):
+        def norm_and_copy(acc, out_row, v_on_vector):
             sumsq = stat_pool.tile([P, 2], F32, name="sumsq")
             for o in (Q, K):
                 squares = stat_pool.tile([P, C], BF16, name="squares")
@@ -139,16 +139,16 @@ def tile_internattention_pa_t_kernel(
                     out=squares[:], in_=acc[o][:], func=ACT.Square, accum_out=sumsq[:, o : o + 1]
                 )
             if v_on_vector:
-                nc.vector.tensor_copy(out=out_sb[V][:, i, :], in_=acc[V][:])
+                nc.vector.tensor_copy(out=out_row[V], in_=acc[V][:])
             else:
-                nc.scalar.copy(out=out_sb[V][:, i, :], in_=acc[V][:])
+                nc.scalar.copy(out=out_row[V], in_=acc[V][:])
             rstd = stat_pool.tile([P, 2], F32, name="rstd")
             nc.scalar.activation(
                 out=rstd[:], in_=sumsq[:], func=ACT.Abs_reciprocal_sqrt, scale=1.0 / C, bias=EPS
             )
             for o in (Q, K):
                 nc.vector.scalar_tensor_tensor(
-                    out=out_sb[o][:, i, :],
+                    out=out_row[o],
                     in0=acc[o][:],
                     scalar=rstd[:, o : o + 1],
                     in1=gains[:, o, :],
@@ -156,11 +156,22 @@ def tile_internattention_pa_t_kernel(
                     op1=ALU.mult,
                 )
 
-        def store(h, out_sb, rows):
-            for o in (V, Q, K):
-                nc.sync.dma_start(
-                    out=out_pairs[o][h // GROUP, h % GROUP][:, rows, :], in_=out_sb[o][:, rows, :]
-                )
+        chunk_of = []
+        for n in STORE_PLAN:
+            chunk_of.extend([(len(chunk_of), n)] * n)
+        out_sb = {}
+
+        def finish(r, acc, v_on_vector):
+            first, n = chunk_of[r]
+            if r == first:
+                for o in (Q, K, V):
+                    out_sb[o] = out_pool.tile([P, STORE_MAX, C], F32, name="out_sb%d" % o)
+            norm_and_copy(acc, [out_sb[o][:, r - first, :] for o in (Q, K, V)], v_on_vector)
+            if r == first + n - 1:
+                for o in (V, Q, K):
+                    nc.sync.dma_start(
+                        out=out_rows[o][:, first : first + n, :], in_=out_sb[o][:, 0:n, :]
+                    )
 
         quantised = {}
         for h in range(AHEAD):
@@ -170,18 +181,13 @@ def tile_internattention_pa_t_kernel(
             quantised[h] = quantise_pair(grouped)
 
         for h in range(PAIRS):
-            out_sb = [out_pool.tile([P, PAIR, C], F32, name="out_sb%d" % o) for o in (Q, K, V)]
             codes, plane = quantised[h]
             later = h + AHEAD
-            norm_and_copy(multiply(codes, plane, 0, (Q, K, V)), 0, out_sb, False)
-            last = h == PAIRS - 1
-            if last:
-                store(h, out_sb, slice(0, 1))
+            finish(PAIR * h, multiply(codes, plane, 0, (Q, K, V)), False)
             acc = multiply(codes, plane, 1, (Q,))
             if later < PAIRS:
                 grouped = regroup_pair(transpose_pair(later))
             acc.extend(multiply(codes, plane, 1, (K, V)))
-            norm_and_copy(acc, 1, out_sb, h % 2 == 0)
+            finish(PAIR * h + 1, acc, h % 2 == 0)
             if later < PAIRS:
                 quantised[later] = quantise_pair(grouped)
-            store(h, out_sb, slice(1, PAIR) if last else slice(0, PAIR))

@@ -20,8 +20,8 @@ EPS = 1e-6
 PAIR = 2
 PAIRS = TOKENS // (PAIR * P)
 TILES = TOKENS // P
-LOAD_PLAN = (2, 2, 4, 8, 8, 8)
-STORE_PLAN = (2, 2, 4, 4, 4, 4, 4, 4, 2, 1, 1)
+LOAD_PLAN = (2, 2) + (4,) * 7
+STORE_PLAN = (2,) * 15 + (1, 1)
 STORE_MAX = max(STORE_PLAN)
 AHEAD = 2
 Q, K, V = 0, 1, 2
@@ -46,7 +46,7 @@ def tile_internattention_pa_t_kernel(
         grouped_pool = stack.enter_context(tc.tile_pool(name="grouped", bufs=2))
         mx_pool = stack.enter_context(tc.tile_pool(name="mx", bufs=AHEAD + 2))
         stat_pool = stack.enter_context(tc.tile_pool(name="stat", bufs=4))
-        out_pool = stack.enter_context(tc.tile_pool(name="out", bufs=5))
+        out_pool = stack.enter_context(tc.tile_pool(name="out", bufs=6))
         psum = stack.enter_context(tc.psum_pool(name="psum", bufs=1))
 
         w_words = const.tile([P, 2 * 3 * C], U8, align_bytes=64)

@@ -21,8 +21,8 @@ PAIR = 2
 PAIRS = TOKENS // (PAIR * P)
 TILES = TOKENS // P
 LOAD_PLAN = (2, 2) + (4,) * 7
-STORE_PLAN = (2,) * 15 + (1, 1)
-STORE_MAX = max(STORE_PLAN)
+STORE_PLANS = ((2,) + (3,) * 10, (3,) * 10 + (2,), (1,) + (3,) * 10 + (1,))
+STORE_MAX = 3
 AHEAD = 2
 Q, K, V = 0, 1, 2
 ACC_BANKS = 7
@@ -157,18 +157,23 @@ def tile_internattention_pa_t_kernel(
                 )
 
         chunk_of = []
-        for n in STORE_PLAN:
-            chunk_of.extend([(len(chunk_of), n)] * n)
+        for plan in STORE_PLANS:
+            chunks = []
+            for n in plan:
+                chunks.extend([(len(chunks), n)] * n)
+            chunk_of.append(chunks)
         out_sb = {}
 
         def finish(r, acc, v_on_vector):
-            first, n = chunk_of[r]
-            if r == first:
-                for o in (Q, K, V):
+            for o in (Q, K, V):
+                if r == chunk_of[o][r][0]:
                     out_sb[o] = out_pool.tile([P, STORE_MAX, C], F32, name="out_sb%d" % o)
-            norm_and_copy(acc, [out_sb[o][:, r - first, :] for o in (Q, K, V)], v_on_vector)
-            if r == first + n - 1:
-                for o in (V, Q, K):
+            norm_and_copy(
+                acc, [out_sb[o][:, r - chunk_of[o][r][0], :] for o in (Q, K, V)], v_on_vector
+            )
+            for o in (V, Q, K):
+                first, n = chunk_of[o][r]
+                if r == first + n - 1:
                     nc.sync.dma_start(
                         out=out_rows[o][:, first : first + n, :], in_=out_sb[o][:, 0:n, :]
                     )

@@ -20,7 +20,7 @@ EPS = 1e-6
 PAIR = 2
 PAIRS = TOKENS // (PAIR * P)
 TILES = TOKENS // P
-LOAD_PLAN = (2, 2) + (4,) * 7
+LOAD_PLAN = (2, 2, 6, 8, 8, 6)
 STORE_PLANS = ((2,) + (3,) * 10, (3,) * 10 + (2,), (1,) + (3,) * 10 + (1,))
 STORE_MAX = 3
 AHEAD = 2
@@ -53,17 +53,18 @@ def tile_internattention_pa_t_kernel(
         w_plane = const.tile([P, 3 * C], U8, align_bytes=64)
         gain_rows = const.tile([P, 2 * C], BF16)
         ones = const.tile([P, P], BF16)
-        gains = const.tile([P, 2, C], F32)
+        gains = const.tile([P, 2, C], BF16)
         ident = const.tile([P, P], F32)
         one_col = const.tile([P, 1], F32)
 
-        nc.vector.memset(gain_rows[:], 0.0)
         nc.vector.memset(w_plane[:].bitcast(I32), 0)
-        nc.vector.memset(ones[:], 1.0)
+        nc.vector.memset(gain_rows[0 : P - 1, :].bitcast(I32), 0)
         nc.vector.memset(one_col[:], 1.0)
+        nc.vector.memset(ones[:], 1.0)
         make_identity(nc, ident[:])
         nc.scalar.activation(out=one_col[:], in_=one_col[:], func=ACT.Abs_reciprocal_sqrt)
 
+        nc.sync.dma_start(out=gain_rows[P - 1 : P, 0:C], in_=q_norm_w.unsqueeze(0))
         x_sb = []
         for j, n in enumerate(LOAD_PLAN):
             first = len(x_sb)
@@ -71,8 +72,7 @@ def tile_internattention_pa_t_kernel(
             nc.sync.dma_start(out=x_j[:], in_=x_rows[:, first : first + n, :])
             x_sb.extend([x_j[:, i, :] for i in range(n)])
             if j == 0:
-                nc.sync.dma_start(out=gain_rows[0:1, 0:C], in_=q_norm_w.unsqueeze(0))
-                nc.sync.dma_start(out=gain_rows[0:1, C : 2 * C], in_=k_norm_w.unsqueeze(0))
+                nc.sync.dma_start(out=gain_rows[P - 1 : P, C : 2 * C], in_=k_norm_w.unsqueeze(0))
                 for quad in range(4):
                     nc.sync.dma_start(
                         out=w_plane[32 * quad : 32 * quad + 4, :].bitcast(I32),
@@ -81,40 +81,44 @@ def tile_internattention_pa_t_kernel(
                 nc.sync.dma_start(out=w_words[:].bitcast(I32), in_=w_qkv_words[0].bitcast(I32))
 
         def spread_gains():
+            gain_ps = psum.tile([P, 2, C], BF16, name="gain_ps", tag="acc", bufs=ACC_BANKS)
             for o in (Q, K):
-                gain_ps = psum.tile([P, C], F32, name="gain_ps", tag="acc", bufs=ACC_BANKS)
                 nc.tensor.matmul(
-                    out=gain_ps[:], lhsT=ones[:], rhs=gain_rows[:, C * o : C * (o + 1)],
+                    out=gain_ps[:, o, :], lhsT=ones[:], rhs=gain_rows[:, C * o : C * (o + 1)],
                     start=True, stop=True,
                 )
-                nc.scalar.copy(out=gains[:, o, :], in_=gain_ps[:])
+            return gain_ps
 
-        def transpose_pair(h):
-            xt = psum.tile([P, PAIR, 2, P], F32, name="xt")
-            for i in range(PAIR):
-                words = x_sb[PAIR * h + i].bitcast(F32)
+        def transpose_unit(tiles, in_acc=False):
+            shape = [P, len(tiles), 2, P]
+            if in_acc:
+                xt = psum.tile(shape, F32, name="xt_acc", tag="acc", bufs=ACC_BANKS)
+            else:
+                xt = psum.tile(shape, F32, name="xt")
+            for i, r in enumerate(tiles):
+                words = x_sb[r].bitcast(F32)
                 for u in range(2):
                     nc.tensor.transpose(xt[:, i, u, :], words[:, u : C // 2 : 2], ident[:])
             return xt
 
-        def regroup_pair(xt):
-            grouped = grouped_pool.tile([P, PAIR, P, 4], BF16, name="grouped", align_bytes=64)
-            nc.vector.tensor_copy(
-                out=grouped[:].bitcast(F32), in_=xt[:].rearrange("p i u r -> p i r u")
-            )
+        def regroup_unit(xt, n, copy):
+            grouped = grouped_pool.tile([P, n, P, 4], BF16, name="grouped", align_bytes=64)
+            copy(out=grouped[:].bitcast(F32), in_=xt[:].rearrange("p i u r -> p i r u"))
             return grouped
 
-        def quantise_pair(grouped):
-            codes = mx_pool.tile([P, PAIR * P], U32, name="codes", align_bytes=64)
-            plane = mx_pool.tile([P, PAIR * P], U8, name="plane", align_bytes=64)
+        def quantise_unit(grouped, n):
+            codes = mx_pool.tile([P, n * P], U32, name="codes", align_bytes=64)
+            plane = mx_pool.tile([P, n * P], U8, name="plane", align_bytes=64)
             nc.vector.quantize_mx(
                 out=codes[:].bitcast(FP8X4),
                 scales=plane[:],
                 in_=grouped[:].rearrange("p i r t -> p (i r t)"),
             )
-            return codes, plane
+            for i in range(n):
+                quantised.append((codes, plane, i))
 
-        def multiply(codes, plane, i, outputs):
+        def multiply(r, outputs):
+            codes, plane, i = quantised[r]
             tokens = slice(P * i, P * (i + 1))
             acc = []
             for o in outputs:
@@ -163,6 +167,7 @@ def tile_internattention_pa_t_kernel(
                 chunks.extend([(len(chunks), n)] * n)
             chunk_of.append(chunks)
         out_sb = {}
+        quantised = []
 
         def finish(r, acc, v_on_vector):
             for o in (Q, K, V):
@@ -178,21 +183,32 @@ def tile_internattention_pa_t_kernel(
                         out=out_rows[o][:, first : first + n, :], in_=out_sb[o][:, 0:n, :]
                     )
 
-        quantised = {}
-        for h in range(AHEAD):
-            grouped = regroup_pair(transpose_pair(h))
-            if h == 0:
-                spread_gains()
-            quantised[h] = quantise_pair(grouped)
+        xt_0 = transpose_unit([0])
+        xt_1 = transpose_unit([1], in_acc=True)
+        gain_ps = spread_gains()
+        grouped_0 = regroup_unit(xt_0, 1, nc.vector.tensor_copy)
+        grouped_1 = regroup_unit(xt_1, 1, nc.scalar.copy)
+        quantise_unit(grouped_0, 1)
+        quantise_unit(grouped_1, 1)
+        nc.vector.tensor_copy(out=gains[:], in_=gain_ps[:])
 
-        for h in range(PAIRS):
-            codes, plane = quantised[h]
-            later = h + AHEAD
-            finish(PAIR * h, multiply(codes, plane, 0, (Q, K, V)), False)
-            acc = multiply(codes, plane, 1, (Q,))
-            if later < PAIRS:
-                grouped = regroup_pair(transpose_pair(later))
-            acc.extend(multiply(codes, plane, 1, (K, V)))
-            finish(PAIR * h + 1, acc, h % 2 == 0)
-            if later < PAIRS:
-                quantised[later] = quantise_pair(grouped)
+        acc_0 = multiply(0, (Q, K, V))
+        grouped = regroup_unit(transpose_unit([2, 3]), 2, nc.vector.tensor_copy)
+        acc_1 = multiply(1, (Q, K, V))
+        xt = transpose_unit([4, 5])
+        quantise_unit(grouped, 2)
+        finish(0, acc_0, False)
+        finish(1, acc_1, True)
+        quantise_unit(regroup_unit(xt, 2, nc.scalar.copy), 2)
+
+        for h in range(1, PAIRS):
+            first = PAIR * h
+            later = list(range(first + PAIR * AHEAD, min(first + PAIR * (AHEAD + 1), TILES)))
+            finish(first, multiply(first, (Q, K, V)), False)
+            acc = multiply(first + 1, (Q,))
+            if later:
+                grouped = regroup_unit(transpose_unit(later), 2, nc.vector.tensor_copy)
+            acc.extend(multiply(first + 1, (K, V)))
+            finish(first + 1, acc, h % 2 == 0)
+            if later:
+                quantise_unit(grouped, 2)

@@ -142,6 +142,8 @@ def tile_internattention_pa_t_kernel(
                 nc.scalar.activation(
                     out=squares[:], in_=acc[o][:], func=ACT.Square, accum_out=sumsq[:, o : o + 1]
                 )
+            if v_due:
+                store(V, v_due.pop(), nc.scalar)
             if v_on_vector:
                 nc.vector.tensor_copy(out=out_row[V], in_=acc[V][:])
             else:
@@ -169,6 +171,12 @@ def tile_internattention_pa_t_kernel(
         out_sb = {}
         quantised = []
 
+        v_due = []
+
+        def store(o, chunk, queue):
+            first, n, tile = chunk
+            queue.dma_start(out=out_rows[o][:, first : first + n, :], in_=tile[:, 0:n, :])
+
         def finish(r, acc, v_on_vector):
             for o in (Q, K, V):
                 if r == chunk_of[o][r][0]:
@@ -179,9 +187,10 @@ def tile_internattention_pa_t_kernel(
             for o in (V, Q, K):
                 first, n = chunk_of[o][r]
                 if r == first + n - 1:
-                    nc.sync.dma_start(
-                        out=out_rows[o][:, first : first + n, :], in_=out_sb[o][:, 0:n, :]
-                    )
+                    if o == V and r < TILES - 1:
+                        v_due.append((first, n, out_sb[V]))
+                    else:
+                        store(o, (first, n, out_sb[o]), nc.sync)
 
         xt_0 = transpose_unit([0])
         xt_1 = transpose_unit([1], in_acc=True)

@@ -57,14 +57,17 @@ def tile_internattention_pa_t_kernel(
         ident = const.tile([P, P], F32)
         one_col = const.tile([P, 1], F32)
 
-        nc.vector.memset(w_plane[:].bitcast(I32), 0)
-        nc.vector.memset(gain_rows[0 : P - 1, :].bitcast(I32), 0)
+        warm = const.tile([P, C], BF16)
         nc.vector.memset(one_col[:], 1.0)
+        nc.vector.memset(w_plane[:].bitcast(I32), 0)
+        nc.vector.memset(warm[:].bitcast(I32), 0)
         nc.vector.memset(ones[:], 1.0)
+        nc.vector.memset(gain_rows[0 : P - 1, :].bitcast(I32), 0)
         make_identity(nc, ident[:])
         nc.scalar.activation(out=one_col[:], in_=one_col[:], func=ACT.Abs_reciprocal_sqrt)
 
         nc.sync.dma_start(out=gain_rows[P - 1 : P, 0:C], in_=q_norm_w.unsqueeze(0))
+        nc.sync.dma_start(out=gain_rows[P - 1 : P, C : 2 * C], in_=k_norm_w.unsqueeze(0))
         x_sb = []
         for j, n in enumerate(LOAD_PLAN):
             first = len(x_sb)
@@ -72,13 +75,12 @@ def tile_internattention_pa_t_kernel(
             nc.sync.dma_start(out=x_j[:], in_=x_rows[:, first : first + n, :])
             x_sb.extend([x_j[:, i, :] for i in range(n)])
             if j == 0:
-                nc.sync.dma_start(out=gain_rows[P - 1 : P, C : 2 * C], in_=k_norm_w.unsqueeze(0))
+                nc.sync.dma_start(out=w_words[:].bitcast(I32), in_=w_qkv_words[0].bitcast(I32))
                 for quad in range(4):
                     nc.sync.dma_start(
                         out=w_plane[32 * quad : 32 * quad + 4, :].bitcast(I32),
                         in_=w_qkv_scales[0, 4 * quad : 4 * quad + 4, :].bitcast(I32),
                     )
-                nc.sync.dma_start(out=w_words[:].bitcast(I32), in_=w_qkv_words[0].bitcast(I32))
 
         def spread_gains():
             gain_ps = psum.tile([P, 2, C], BF16, name="gain_ps", tag="acc", bufs=ACC_BANKS)
@@ -192,9 +194,16 @@ def tile_internattention_pa_t_kernel(
                     else:
                         store(o, (first, n, out_sb[o]), nc.sync)
 
+        warm_ps = psum.tile([P, C], F32, name="warm_ps", tag="acc", bufs=ACC_BANKS)
+        for i in range(2):
+            nc.tensor.matmul(
+                out=warm_ps[:], lhsT=warm[:, 0:P], rhs=warm[:], start=True, stop=True
+            )
+
+        gain_ps = spread_gains()
+
         xt_0 = transpose_unit([0])
         xt_1 = transpose_unit([1], in_acc=True)
-        gain_ps = spread_gains()
         grouped_0 = regroup_unit(xt_0, 1, nc.vector.tensor_copy)
         grouped_1 = regroup_unit(xt_1, 1, nc.scalar.copy)
         quantise_unit(grouped_0, 1)

@@ -154,6 +154,8 @@ def tile_internattention_pa_t_kernel(
             nc.scalar.activation(
                 out=rstd[:], in_=sumsq[:], func=ACT.Abs_reciprocal_sqrt, scale=1.0 / C, bias=EPS
             )
+            if q_due:
+                store(Q, q_due.pop(), nc.scalar)
             for o in (Q, K):
                 nc.vector.scalar_tensor_tensor(
                     out=out_row[o],
@@ -173,6 +175,7 @@ def tile_internattention_pa_t_kernel(
         out_sb = {}
         quantised = []
 
+        q_due = []
         v_due = []
 
         def store(o, chunk, queue):
@@ -191,6 +194,8 @@ def tile_internattention_pa_t_kernel(
                 if r == first + n - 1:
                     if o == V and r < TILES - 1:
                         v_due.append((first, n, out_sb[V]))
+                    elif o == Q and r % 2 == 0:
+                        q_due.append((first, n, out_sb[Q]))
                     else:
                         store(o, (first, n, out_sb[o]), nc.sync)
 

@@ -20,7 +20,7 @@ EPS = 1e-6
 PAIR = 2
 PAIRS = TOKENS // (PAIR * P)
 TILES = TOKENS // P
-LOAD_PLAN = (2, 2, 6, 8, 8, 6)
+LOAD_PLAN = (2, 2, 6, 22)
 STORE_PLANS = ((2,) + (3,) * 10, (3,) * 10 + (2,), (1,) + (3,) * 10 + (1,))
 STORE_MAX = 3
 AHEAD = 2
@@ -137,7 +137,7 @@ def tile_internattention_pa_t_kernel(
                 acc.append(acc_o)
             return acc
 
-        def norm_and_copy(acc, out_row, v_on_vector):
+        def norm_and_copy(acc, out_row, v_on_vector, v_first):
             sumsq = stat_pool.tile([P, 2], F32, name="sumsq")
             for o in (Q, K):
                 squares = stat_pool.tile([P, C], BF16, name="squares")
@@ -146,10 +146,10 @@ def tile_internattention_pa_t_kernel(
                 )
             if v_due:
                 store(V, v_due.pop(), nc.scalar)
-            if v_on_vector:
-                nc.vector.tensor_copy(out=out_row[V], in_=acc[V][:])
-            else:
+            if not v_on_vector:
                 nc.scalar.copy(out=out_row[V], in_=acc[V][:])
+            elif v_first:
+                nc.vector.tensor_copy(out=out_row[V], in_=acc[V][:])
             rstd = stat_pool.tile([P, 2], F32, name="rstd")
             nc.scalar.activation(
                 out=rstd[:], in_=sumsq[:], func=ACT.Abs_reciprocal_sqrt, scale=1.0 / C, bias=EPS
@@ -165,6 +165,8 @@ def tile_internattention_pa_t_kernel(
                     op0=ALU.mult,
                     op1=ALU.mult,
                 )
+            if v_on_vector and not v_first:
+                nc.vector.tensor_copy(out=out_row[V], in_=acc[V][:])
 
         chunk_of = []
         for plan in STORE_PLANS:
@@ -187,7 +189,8 @@ def tile_internattention_pa_t_kernel(
                 if r == chunk_of[o][r][0]:
                     out_sb[o] = out_pool.tile([P, STORE_MAX, C], F32, name="out_sb%d" % o)
             norm_and_copy(
-                acc, [out_sb[o][:, r - chunk_of[o][r][0], :] for o in (Q, K, V)], v_on_vector
+                acc, [out_sb[o][:, r - chunk_of[o][r][0], :] for o in (Q, K, V)], v_on_vector,
+                r == sum(chunk_of[V][r]) - 1,
             )
             for o in (V, Q, K):
                 first, n = chunk_of[o][r]

@@ -195,7 +195,9 @@ def tile_internattention_pa_t_kernel(
             for o in (V, Q, K):
                 first, n = chunk_of[o][r]
                 if r == first + n - 1:
-                    if o == V and r < TILES - 1:
+                    if r == TILES - 1:
+                        store(o, (first, n, out_sb[o]), nc.sync if o == Q else nc.scalar)
+                    elif o == V:
                         v_due.append((first, n, out_sb[V]))
                     elif o == Q and r % 2 == 0:
                         q_due.append((first, n, out_sb[Q]))

from contextlib import ExitStack

import concourse.mybir as mybir
from concourse.masks import make_identity

F32 = mybir.dt.float32
BF16 = mybir.dt.bfloat16
I32 = mybir.dt.int32
U32 = mybir.dt.uint32
U8 = mybir.dt.uint8
FP8X4 = mybir.dt.float8_e4m3fn_x4
FP4X4 = mybir.dt.float4_e2m1fn_x4
ACT = mybir.ActivationFunctionType
ALU = mybir.AluOpType

P = 128
C = 512
TOKENS = 4 * 1024
EPS = 1e-6
PAIR = 2
PAIRS = TOKENS // (PAIR * P)
TILES = TOKENS // P
LOAD_PLAN = (2, 2, 6, 22)
STORE_PLANS = ((2,) + (3,) * 10, (3,) * 10 + (2,), (1,) + (3,) * 10 + (1,))
STORE_MAX = 3
AHEAD = 2
Q, K, V = 0, 1, 2
ACC_BANKS = 7

FLOPS = 2 * TOKENS * C * 3 * C


def tile_internattention_pa_t_kernel(
    tc, x, w_qkv_words, w_qkv_scales, q_norm_w, k_norm_w, out_0, out_1, out_2
):
    nc = tc.nc
    x_rows = x.flatten_outer_dims().rearrange("(p r) c -> p r c", p=P)
    out_rows = [
        o.flatten_outer_dims().rearrange("(p r) c -> p r c", p=P) for o in (out_0, out_1, out_2)
    ]

    with ExitStack() as stack:
        stack.enter_context(tc.manual_schedule())
        const = stack.enter_context(tc.tile_pool(name="const", bufs=1))
        x_pool = stack.enter_context(tc.tile_pool(name="x", bufs=1))
        grouped_pool = stack.enter_context(tc.tile_pool(name="grouped", bufs=2))
        mx_pool = stack.enter_context(tc.tile_pool(name="mx", bufs=AHEAD + 2))
        stat_pool = stack.enter_context(tc.tile_pool(name="stat", bufs=4))
        out_pool = stack.enter_context(tc.tile_pool(name="out", bufs=6))
        psum = stack.enter_context(tc.psum_pool(name="psum", bufs=1))

        w_words = const.tile([P, 2 * 3 * C], U8, align_bytes=64)
        w_plane = const.tile([P, 3 * C], U8, align_bytes=64)
        gain_rows = const.tile([P, 2 * C], BF16)
        ones = const.tile([P, P], BF16)
        gains = const.tile([P, 2, C], BF16)
        ident = const.tile([P, P], F32)
        one_col = const.tile([P, 1], F32)

        warm = const.tile([P, C], BF16)
        nc.vector.memset(one_col[:], 1.0)
        nc.vector.memset(w_plane[:].bitcast(I32), 0)
        nc.vector.memset(warm[:].bitcast(I32), 0)
        nc.vector.memset(ones[:], 1.0)
        nc.vector.memset(gain_rows[0 : P - 1, :].bitcast(I32), 0)
        make_identity(nc, ident[:])
        nc.scalar.activation(out=one_col[:], in_=one_col[:], func=ACT.Abs_reciprocal_sqrt)

        nc.sync.dma_start(out=gain_rows[P - 1 : P, 0:C], in_=q_norm_w.unsqueeze(0))
        nc.sync.dma_start(out=gain_rows[P - 1 : P, C : 2 * C], in_=k_norm_w.unsqueeze(0))
        x_sb = []
        for j, n in enumerate(LOAD_PLAN):
            first = len(x_sb)
            x_j = x_pool.tile([P, n, C], BF16, name="x_%d" % j)
            nc.sync.dma_start(out=x_j[:], in_=x_rows[:, first : first + n, :])
            x_sb.extend([x_j[:, i, :] for i in range(n)])
            if j == 0:
                nc.sync.dma_start(out=w_words[:].bitcast(I32), in_=w_qkv_words[0].bitcast(I32))
                for quad in range(4):
                    nc.sync.dma_start(
                        out=w_plane[32 * quad : 32 * quad + 4, :].bitcast(I32),
                        in_=w_qkv_scales[0, 4 * quad : 4 * quad + 4, :].bitcast(I32),
                    )

        def spread_gains():
            gain_ps = psum.tile([P, 2, C], BF16, name="gain_ps", tag="acc", bufs=ACC_BANKS)
            for o in (Q, K):
                nc.tensor.matmul(
                    out=gain_ps[:, o, :], lhsT=ones[:], rhs=gain_rows[:, C * o : C * (o + 1)],
                    start=True, stop=True,
                )
            return gain_ps

        def transpose_unit(tiles, in_acc=False):
            shape = [P, len(tiles), 2, P]
            if in_acc:
                xt = psum.tile(shape, F32, name="xt_acc", tag="acc", bufs=ACC_BANKS)
            else:
                xt = psum.tile(shape, F32, name="xt")
            for i, r in enumerate(tiles):
                words = x_sb[r].bitcast(F32)
                for u in range(2):
                    nc.tensor.transpose(xt[:, i, u, :], words[:, u : C // 2 : 2], ident[:])
            return xt

        def regroup_unit(xt, n, copy):
            grouped = grouped_pool.tile([P, n, P, 4], BF16, name="grouped", align_bytes=64)
            copy(out=grouped[:].bitcast(F32), in_=xt[:].rearrange("p i u r -> p i r u"))
            return grouped

        def quantise_unit(grouped, n):
            codes = mx_pool.tile([P, n * P], U32, name="codes", align_bytes=64)
            plane = mx_pool.tile([P, n * P], U8, name="plane", align_bytes=64)
            nc.vector.quantize_mx(
                out=codes[:].bitcast(FP8X4),
                scales=plane[:],
                in_=grouped[:].rearrange("p i r t -> p (i r t)"),
            )
            for i in range(n):
                quantised.append((codes, plane, i))

        def multiply(r, outputs):
            codes, plane, i = quantised[r]
            tokens = slice(P * i, P * (i + 1))
            acc = []
            for o in outputs:
                acc_o = psum.tile([P, C], F32, name="acc_o", tag="acc", bufs=ACC_BANKS)
                nc.tensor.matmul_mx(
                    out=acc_o[:],
                    lhsT=codes[:, tokens].bitcast(FP8X4),
                    lhsT_scale=plane[:, tokens],
                    rhs=w_words[:, 2 * C * o : 2 * C * (o + 1)].bitcast(FP4X4),
                    rhs_scale=w_plane[:, C * o : C * (o + 1)],
                    start=True,
                    stop=True,
                )
                acc.append(acc_o)
            return acc

        def norm_and_copy(acc, out_row, v_on_vector, v_first):
            sumsq = stat_pool.tile([P, 2], F32, name="sumsq")
            for o in (Q, K):
                squares = stat_pool.tile([P, C], BF16, name="squares")
                nc.scalar.activation(
                    out=squares[:], in_=acc[o][:], func=ACT.Square, accum_out=sumsq[:, o : o + 1]
                )
            if v_due:
                store(V, v_due.pop(), nc.scalar)
            if not v_on_vector:
                nc.scalar.copy(out=out_row[V], in_=acc[V][:])
            elif v_first:
                nc.vector.tensor_copy(out=out_row[V], in_=acc[V][:])
            rstd = stat_pool.tile([P, 2], F32, name="rstd")
            nc.scalar.activation(
                out=rstd[:], in_=sumsq[:], func=ACT.Abs_reciprocal_sqrt, scale=1.0 / C, bias=EPS
            )
            if q_due:
                store(Q, q_due.pop(), nc.scalar)
            for o in (Q, K):
                nc.vector.scalar_tensor_tensor(
                    out=out_row[o],
                    in0=acc[o][:],
                    scalar=rstd[:, o : o + 1],
                    in1=gains[:, o, :],
                    op0=ALU.mult,
                    op1=ALU.mult,
                )
            if v_on_vector and not v_first:
                nc.vector.tensor_copy(out=out_row[V], in_=acc[V][:])

        chunk_of = []
        for plan in STORE_PLANS:
            chunks = []
            for n in plan:
                chunks.extend([(len(chunks), n)] * n)
            chunk_of.append(chunks)
        out_sb = {}
        quantised = []

        q_due = []
        v_due = []

        def store(o, chunk, queue):
            first, n, tile = chunk
            queue.dma_start(out=out_rows[o][:, first : first + n, :], in_=tile[:, 0:n, :])

        def finish(r, acc, v_on_vector):
            for o in (Q, K, V):
                if r == chunk_of[o][r][0]:
                    out_sb[o] = out_pool.tile([P, STORE_MAX, C], F32, name="out_sb%d" % o)
            norm_and_copy(
                acc, [out_sb[o][:, r - chunk_of[o][r][0], :] for o in (Q, K, V)], v_on_vector,
                r == sum(chunk_of[V][r]) - 1,
            )
            for o in (V, Q, K):
                first, n = chunk_of[o][r]
                if r == first + n - 1:
                    if r == TILES - 1:
                        store(o, (first, n, out_sb[o]), nc.sync if o == Q else nc.scalar)
                    elif o == V:
                        v_due.append((first, n, out_sb[V]))
                    elif o == Q and r % 2 == 0:
                        q_due.append((first, n, out_sb[Q]))
                    else:
                        store(o, (first, n, out_sb[o]), nc.sync)

        warm_ps = psum.tile([P, C], F32, name="warm_ps", tag="acc", bufs=ACC_BANKS)
        for i in range(2):
            nc.tensor.matmul(
                out=warm_ps[:], lhsT=warm[:, 0:P], rhs=warm[:], start=True, stop=True
            )

        gain_ps = spread_gains()

        xt_0 = transpose_unit([0])
        xt_1 = transpose_unit([1], in_acc=True)
        grouped_0 = regroup_unit(xt_0, 1, nc.vector.tensor_copy)
        grouped_1 = regroup_unit(xt_1, 1, nc.scalar.copy)
        quantise_unit(grouped_0, 1)
        quantise_unit(grouped_1, 1)
        nc.vector.tensor_copy(out=gains[:], in_=gain_ps[:])

        acc_0 = multiply(0, (Q, K, V))
        grouped = regroup_unit(transpose_unit([2, 3]), 2, nc.vector.tensor_copy)
        acc_1 = multiply(1, (Q, K, V))
        xt = transpose_unit([4, 5])
        quantise_unit(grouped, 2)
        finish(0, acc_0, False)
        finish(1, acc_1, True)
        quantise_unit(regroup_unit(xt, 2, nc.scalar.copy), 2)

        for h in range(1, PAIRS):
            first = PAIR * h
            later = list(range(first + PAIR * AHEAD, min(first + PAIR * (AHEAD + 1), TILES)))
            finish(first, multiply(first, (Q, K, V)), False)
            acc = multiply(first + 1, (Q,))
            if later:
                grouped = regroup_unit(transpose_unit(later), 2, nc.vector.tensor_copy)
            acc.extend(multiply(first + 1, (K, V)))
            finish(first + 1, acc, h % 2 == 0)
            if later:
                quantise_unit(grouped, 2)
